import numpy as np
import ml_dtypes

BF16 = ml_dtypes.bfloat16


def bf(x):
    return np.asarray(x, np.float32).astype(BF16)


def f32(x):
    return np.asarray(x, np.float32)


def f64(x):
    return np.asarray(x).astype(np.float64)


def striped(idx):
    return np.tile(idx.reshape(-1, 16).T, (8, 1))


D, S, M, N = 128, 1024, 128, 512


def setup_inputs():
    return {'table': bf(0.25 * np.random.standard_normal((D, S))), 'x': bf(0.25 * np.random.standard_normal((D, M))), 'offs': striped(np.random.permutation(np.tile(np.arange(S), 2))[:N])}


def reference(table, x, offs):
    idx = offs[:16].T.reshape(-1)
    nf = f64(table)[:, idx]
    xq = f64(x)
    x2 = np.sum(xq * xq, axis=0)[:, None]
    t2 = np.sum(nf * nf, axis=0)[None, :]
    return np.sqrt(x2 + t2 - 2.0 * (xq.T @ nf))

@@ -1,0 +1,62 @@
+import concourse.mybir as mybir
+from concourse.masks import make_identity
+
+D, S, M, N = 128, 1024, 128, 512
+FLOPS = 2 * D * M * N
+BYTES = 2 * D * N + 2 * D * M + 2 * N + 4 * M * N
+
+BF16, F32, U16 = mybir.dt.bfloat16, mybir.dt.float32, mybir.dt.uint16
+MULT, MAX = mybir.AluOpType.mult, mybir.AluOpType.max
+SQRT, SQUARE = mybir.ActivationFunctionType.Sqrt, mybir.ActivationFunctionType.Square
+
+PIECE = 256
+PIECES = N // PIECE
+SQRT_FLOOR = 2.0**-116
+
+
+def tile_loss_kernel(tc, table, x, offs, out):
+    nc = tc.nc
+    with (
+        tc.tile_pool(name="held", bufs=1) as held,
+        tc.psum_pool(name="psum", bufs=1) as psum,
+    ):
+        offsets = held.tile([128, N // 16], U16, name="offsets")
+        nc.sync.dma_start(offsets[:], offs)
+        table_sb = held.tile([D, S], BF16, name="table_sb")
+        nc.scalar.dma_start(table_sb[:], table)
+        x_sb = held.tile([D, M], BF16, name="x_sb")
+        nc.sync.dma_start(x_sb[:], x)
+
+        scratch = held.tile([128, 1], F32, name="scratch")
+        nc.vector.memset(scratch[:], 1.0)
+        nc.scalar.activation(scratch[:], scratch[:], SQRT)
+
+        identity = held.tile([D, D], BF16, name="identity")
+        make_identity(nc, identity[:])
+        minus_half = held.tile([D, PIECE], BF16, name="minus_half")
+        nc.vector.memset(minus_half[:], -0.5)
+        x_sq = held.tile([D, M], BF16, name="x_sq")
+        nc.vector.tensor_tensor(x_sq[:], x_sb[:], x_sb[:], MULT)
+
+        picked = [psum.tile([D, PIECE], F32, name=f"picked{p}") for p in range(PIECES)]
+        acc = [psum.tile([M, PIECE], F32, name=f"acc{p}") for p in range(PIECES)]
+        piece_offsets = [offsets[:, p * (PIECE // 16) : (p + 1) * (PIECE // 16)] for p in range(PIECES)]
+
+        for p in range(PIECES):
+            nc.tensor.matmul(acc[p][:], x_sq[:], minus_half[:], start=True, stop=False)
+        for p in range(PIECES):
+            nc.tensor.matmul(picked[p][:], identity[:], table_sb[:].indirect(piece_offsets[p]), start=True, stop=True)
+        for p in range(PIECES):
+            nc.tensor.matmul(acc[p][:], x_sb[:], table_sb[:].indirect(piece_offsets[p]), start=False, stop=False)
+
+        picked_sq = held.tile([D, N], BF16, name="picked_sq")
+        dist = held.tile([M, N], F32, name="dist")
+        for p in range(PIECES):
+            columns = slice(p * PIECE, (p + 1) * PIECE)
+            nc.scalar.activation(picked_sq[:, columns], picked[p][:], SQUARE)
+            nc.tensor.matmul(acc[p][:], minus_half[:, :M], picked_sq[:, columns], start=False, stop=True)
+        for p in range(PIECES):
+            columns = slice(p * PIECE, (p + 1) * PIECE)
+            nc.vector.tensor_scalar(dist[:, columns], acc[p][:], -2.0, SQRT_FLOOR, MULT, MAX)
+            nc.scalar.activation(dist[:, columns], dist[:, columns], SQRT)
+            nc.sync.dma_start(out[:, columns], dist[:, columns])

@@ -11,6 +11,7 @@ SQRT, SQUARE = mybir.ActivationFunctionType.Sqrt, mybir.ActivationFunctionType.S
 
 PIECE = 256
 PIECES = N // PIECE
+WARM_UP = 8
 SQRT_FLOOR = 2.0**-116
 
 
@@ -37,6 +38,10 @@ def tile_loss_kernel(tc, table, x, offs, out):
         nc.vector.memset(minus_half[:], -0.5)
         x_sq = held.tile([D, M], BF16, name="x_sq")
         nc.vector.tensor_tensor(x_sq[:], x_sb[:], x_sb[:], MULT)
+
+        warm = psum.tile([M, PIECE], F32, name="warm")
+        for i in range(WARM_UP):
+            nc.tensor.matmul(warm[:], minus_half[:, :M], minus_half[:], start=True, stop=True)
 
         picked = [psum.tile([D, PIECE], F32, name=f"picked{p}") for p in range(PIECES)]
         acc = [psum.tile([M, PIECE], F32, name=f"acc{p}") for p in range(PIECES)]

@@ -9,9 +9,10 @@ BF16, F32, U16 = mybir.dt.bfloat16, mybir.dt.float32, mybir.dt.uint16
 MULT, MAX = mybir.AluOpType.mult, mybir.AluOpType.max
 SQRT, SQUARE = mybir.ActivationFunctionType.Sqrt, mybir.ActivationFunctionType.Square
 
-PIECE = 256
+BANK = 512
+PIECE = 128
 PIECES = N // PIECE
-WARM_UP = 8
+WARM_UP = 4
 SQRT_FLOOR = 2.0**-116
 
 
@@ -28,40 +29,43 @@ def tile_loss_kernel(tc, table, x, offs, out):
         x_sb = held.tile([D, M], BF16, name="x_sb")
         nc.sync.dma_start(x_sb[:], x)
 
+        minus_half = held.tile([D, BANK], BF16, name="minus_half")
+        nc.vector.memset(minus_half[:], -0.5)
+        identity = held.tile([D, D], BF16, name="identity")
+        make_identity(nc, identity[:])
+
         scratch = held.tile([128, 1], F32, name="scratch")
         nc.vector.memset(scratch[:], 1.0)
         nc.scalar.activation(scratch[:], scratch[:], SQRT)
 
-        identity = held.tile([D, D], BF16, name="identity")
-        make_identity(nc, identity[:])
-        minus_half = held.tile([D, PIECE], BF16, name="minus_half")
-        nc.vector.memset(minus_half[:], -0.5)
-        x_sq = held.tile([D, M], BF16, name="x_sq")
-        nc.vector.tensor_tensor(x_sq[:], x_sb[:], x_sb[:], MULT)
-
-        warm = psum.tile([M, PIECE], F32, name="warm")
-        for i in range(WARM_UP):
-            nc.tensor.matmul(warm[:], minus_half[:, :M], minus_half[:], start=True, stop=True)
-
-        picked = [psum.tile([D, PIECE], F32, name=f"picked{p}") for p in range(PIECES)]
-        acc = [psum.tile([M, PIECE], F32, name=f"acc{p}") for p in range(PIECES)]
+        picked = [psum.tile([D, BANK], F32, name=f"picked{p}") for p in range(PIECES)]
+        acc = [psum.tile([M, BANK], F32, name=f"acc{p}") for p in range(PIECES)]
         piece_offsets = [offsets[:, p * (PIECE // 16) : (p + 1) * (PIECE // 16)] for p in range(PIECES)]
 
+        for i in range(WARM_UP):
+            nc.tensor.matmul(acc[0][:], minus_half[:, :M], minus_half[:], start=True, stop=True)
+
+        x_sq = held.tile([D, M], BF16, name="x_sq")
+        nc.vector.tensor_tensor(x_sq[:], x_sb[:], x_sb[:], MULT)
         for p in range(PIECES):
-            nc.tensor.matmul(acc[p][:], x_sq[:], minus_half[:], start=True, stop=False)
+            nc.tensor.matmul(acc[p][:, :PIECE], x_sq[:], minus_half[:, :PIECE], start=True, stop=False)
         for p in range(PIECES):
-            nc.tensor.matmul(picked[p][:], identity[:], table_sb[:].indirect(piece_offsets[p]), start=True, stop=True)
+            nc.tensor.matmul(
+                picked[p][:, :PIECE], identity[:], table_sb[:].indirect(piece_offsets[p]), start=True, stop=True
+            )
         for p in range(PIECES):
-            nc.tensor.matmul(acc[p][:], x_sb[:], table_sb[:].indirect(piece_offsets[p]), start=False, stop=False)
+            nc.tensor.matmul(
+                acc[p][:, :PIECE], x_sb[:], table_sb[:].indirect(piece_offsets[p]), start=False, stop=False
+            )
 
         picked_sq = held.tile([D, N], BF16, name="picked_sq")
         dist = held.tile([M, N], F32, name="dist")
         for p in range(PIECES):
             columns = slice(p * PIECE, (p + 1) * PIECE)
-            nc.scalar.activation(picked_sq[:, columns], picked[p][:], SQUARE)
-            nc.tensor.matmul(acc[p][:], minus_half[:, :M], picked_sq[:, columns], start=False, stop=True)
+            nc.scalar.activation(picked_sq[:, columns], picked[p][:, :PIECE], SQUARE)
+            nc.tensor.matmul(acc[p][:, :PIECE], minus_half[:, :M], picked_sq[:, columns], start=False, stop=True)
         for p in range(PIECES):
             columns = slice(p * PIECE, (p + 1) * PIECE)
-            nc.vector.tensor_scalar(dist[:, columns], acc[p][:], -2.0, SQRT_FLOOR, MULT, MAX)
+            nc.vector.tensor_scalar(dist[:, columns], acc[p][:, :PIECE], -2.0, SQRT_FLOOR, MULT, MAX)
             nc.scalar.activation(dist[:, columns], dist[:, columns], SQRT)
             nc.sync.dma_start(out[:, columns], dist[:, columns])

@@ -1,5 +1,4 @@
 import concourse.mybir as mybir
-from concourse.masks import make_identity
 
 D, S, M, N = 128, 1024, 128, 512
 FLOPS = 2 * D * M * N
@@ -7,7 +6,7 @@ BYTES = 2 * D * N + 2 * D * M + 2 * N + 4 * M * N
 
 BF16, F32, U16 = mybir.dt.bfloat16, mybir.dt.float32, mybir.dt.uint16
 MULT, MAX = mybir.AluOpType.mult, mybir.AluOpType.max
-SQRT, SQUARE = mybir.ActivationFunctionType.Sqrt, mybir.ActivationFunctionType.Square
+SQRT = mybir.ActivationFunctionType.Sqrt
 
 BANK = 512
 PIECE = 128
@@ -31,41 +30,34 @@ def tile_loss_kernel(tc, table, x, offs, out):
 
         minus_half = held.tile([D, BANK], BF16, name="minus_half")
         nc.vector.memset(minus_half[:], -0.5)
-        identity = held.tile([D, D], BF16, name="identity")
-        make_identity(nc, identity[:])
 
         scratch = held.tile([128, 1], F32, name="scratch")
         nc.vector.memset(scratch[:], 1.0)
         nc.scalar.activation(scratch[:], scratch[:], SQRT)
 
-        picked = [psum.tile([D, BANK], F32, name=f"picked{p}") for p in range(PIECES)]
-        acc = [psum.tile([M, BANK], F32, name=f"acc{p}") for p in range(PIECES)]
-        piece_offsets = [offsets[:, p * (PIECE // 16) : (p + 1) * (PIECE // 16)] for p in range(PIECES)]
-
+        warm = psum.tile([M, BANK], F32, name="warm")
         for i in range(WARM_UP):
-            nc.tensor.matmul(acc[0][:], minus_half[:, :M], minus_half[:], start=True, stop=True)
+            nc.tensor.matmul(warm[:], minus_half[:, :M], minus_half[:], start=True, stop=True)
 
         x_sq = held.tile([D, M], BF16, name="x_sq")
         nc.vector.tensor_tensor(x_sq[:], x_sb[:], x_sb[:], MULT)
+        table_sq = held.tile([D, S], BF16, name="table_sq")
+        nc.vector.tensor_tensor(table_sq[:], table_sb[:], table_sb[:], MULT)
+
+        acc = [psum.tile([M, PIECE], F32, name=f"acc{p}") for p in range(PIECES)]
+        piece_offsets = [offsets[:, p * (PIECE // 16) : (p + 1) * (PIECE // 16)] for p in range(PIECES)]
         for p in range(PIECES):
-            nc.tensor.matmul(acc[p][:, :PIECE], x_sq[:], minus_half[:, :PIECE], start=True, stop=False)
+            nc.tensor.matmul(acc[p][:], x_sq[:], minus_half[:, :PIECE], start=True, stop=False)
+        for p in range(PIECES):
+            nc.tensor.matmul(acc[p][:], x_sb[:], table_sb[:].indirect(piece_offsets[p]), start=False, stop=False)
         for p in range(PIECES):
             nc.tensor.matmul(
-                picked[p][:, :PIECE], identity[:], table_sb[:].indirect(piece_offsets[p]), start=True, stop=True
-            )
-        for p in range(PIECES):
-            nc.tensor.matmul(
-                acc[p][:, :PIECE], x_sb[:], table_sb[:].indirect(piece_offsets[p]), start=False, stop=False
+                acc[p][:], minus_half[:, :M], table_sq[:].indirect(piece_offsets[p]), start=False, stop=True
             )
 
-        picked_sq = held.tile([D, N], BF16, name="picked_sq")
         dist = held.tile([M, N], F32, name="dist")
         for p in range(PIECES):
             columns = slice(p * PIECE, (p + 1) * PIECE)
-            nc.scalar.activation(picked_sq[:, columns], picked[p][:, :PIECE], SQUARE)
-            nc.tensor.matmul(acc[p][:, :PIECE], minus_half[:, :M], picked_sq[:, columns], start=False, stop=True)
-        for p in range(PIECES):
-            columns = slice(p * PIECE, (p + 1) * PIECE)
-            nc.vector.tensor_scalar(dist[:, columns], acc[p][:, :PIECE], -2.0, SQRT_FLOOR, MULT, MAX)
+            nc.vector.tensor_scalar(dist[:, columns], acc[p][:], -2.0, SQRT_FLOOR, MULT, MAX)
             nc.scalar.activation(dist[:, columns], dist[:, columns], SQRT)
             nc.sync.dma_start(out[:, columns], dist[:, columns])

@@ -24,7 +24,9 @@ def tile_loss_kernel(tc, table, x, offs, out):
         offsets = held.tile([128, N // 16], U16, name="offsets")
         nc.sync.dma_start(offsets[:], offs)
         table_sb = held.tile([D, S], BF16, name="table_sb")
-        nc.scalar.dma_start(table_sb[:], table)
+        for h in range(2):
+            half = slice(h * (S // 2), (h + 1) * (S // 2))
+            nc.scalar.dma_start(table_sb[:, half], table[:, half])
         x_sb = held.tile([D, M], BF16, name="x_sb")
         nc.sync.dma_start(x_sb[:], x)
 
@@ -42,7 +44,9 @@ def tile_loss_kernel(tc, table, x, offs, out):
         x_sq = held.tile([D, M], BF16, name="x_sq")
         nc.vector.tensor_tensor(x_sq[:], x_sb[:], x_sb[:], MULT)
         table_sq = held.tile([D, S], BF16, name="table_sq")
-        nc.vector.tensor_tensor(table_sq[:], table_sb[:], table_sb[:], MULT)
+        for h in range(2):
+            half = slice(h * (S // 2), (h + 1) * (S // 2))
+            nc.vector.tensor_tensor(table_sq[:, half], table_sb[:, half], table_sb[:, half], MULT)
 
         acc = [psum.tile([M, PIECE], F32, name=f"acc{p}") for p in range(PIECES)]
         piece_offsets = [offsets[:, p * (PIECE // 16) : (p + 1) * (PIECE // 16)] for p in range(PIECES)]

@@ -8,10 +8,8 @@ BF16, F32, U16 = mybir.dt.bfloat16, mybir.dt.float32, mybir.dt.uint16
 MULT, MAX = mybir.AluOpType.mult, mybir.AluOpType.max
 SQRT = mybir.ActivationFunctionType.Sqrt
 
-BANK = 512
 PIECE = 128
 PIECES = N // PIECE
-WARM_UP = 4
 SQRT_FLOOR = 2.0**-116
 
 
@@ -30,16 +28,12 @@ def tile_loss_kernel(tc, table, x, offs, out):
         x_sb = held.tile([D, M], BF16, name="x_sb")
         nc.sync.dma_start(x_sb[:], x)
 
-        minus_half = held.tile([D, BANK], BF16, name="minus_half")
+        minus_half = held.tile([D, PIECE], BF16, name="minus_half")
         nc.vector.memset(minus_half[:], -0.5)
 
         scratch = held.tile([128, 1], F32, name="scratch")
         nc.vector.memset(scratch[:], 1.0)
         nc.scalar.activation(scratch[:], scratch[:], SQRT)
-
-        warm = psum.tile([M, BANK], F32, name="warm")
-        for i in range(WARM_UP):
-            nc.tensor.matmul(warm[:], minus_half[:, :M], minus_half[:], start=True, stop=True)
 
         x_sq = held.tile([D, M], BF16, name="x_sq")
         nc.vector.tensor_tensor(x_sq[:], x_sb[:], x_sb[:], MULT)
@@ -51,12 +45,12 @@ def tile_loss_kernel(tc, table, x, offs, out):
         acc = [psum.tile([M, PIECE], F32, name=f"acc{p}") for p in range(PIECES)]
         piece_offsets = [offsets[:, p * (PIECE // 16) : (p + 1) * (PIECE // 16)] for p in range(PIECES)]
         for p in range(PIECES):
-            nc.tensor.matmul(acc[p][:], x_sq[:], minus_half[:, :PIECE], start=True, stop=False)
+            nc.tensor.matmul(acc[p][:], x_sq[:], minus_half[:], start=True, stop=False)
         for p in range(PIECES):
             nc.tensor.matmul(acc[p][:], x_sb[:], table_sb[:].indirect(piece_offsets[p]), start=False, stop=False)
         for p in range(PIECES):
             nc.tensor.matmul(
-                acc[p][:], minus_half[:, :M], table_sq[:].indirect(piece_offsets[p]), start=False, stop=True
+                acc[p][:], minus_half[:], table_sq[:].indirect(piece_offsets[p]), start=False, stop=True
             )
 
         dist = held.tile([M, N], F32, name="dist")

@@ -8,8 +8,10 @@ BF16, F32, U16 = mybir.dt.bfloat16, mybir.dt.float32, mybir.dt.uint16
 MULT, MAX = mybir.AluOpType.mult, mybir.AluOpType.max
 SQRT = mybir.ActivationFunctionType.Sqrt
 
+BANK = 512
 PIECE = 128
 PIECES = N // PIECE
+WARM_UP = 8
 SQRT_FLOOR = 2.0**-116
 
 
@@ -28,12 +30,16 @@ def tile_loss_kernel(tc, table, x, offs, out):
         x_sb = held.tile([D, M], BF16, name="x_sb")
         nc.sync.dma_start(x_sb[:], x)
 
-        minus_half = held.tile([D, PIECE], BF16, name="minus_half")
+        minus_half = held.tile([D, BANK], BF16, name="minus_half")
         nc.vector.memset(minus_half[:], -0.5)
 
         scratch = held.tile([128, 1], F32, name="scratch")
         nc.vector.memset(scratch[:], 1.0)
         nc.scalar.activation(scratch[:], scratch[:], SQRT)
+
+        warm = psum.tile([M, BANK], F32, name="warm")
+        for i in range(WARM_UP):
+            nc.tensor.matmul(warm[:], minus_half[:, :M], minus_half[:], start=True, stop=True)
 
         x_sq = held.tile([D, M], BF16, name="x_sq")
         nc.vector.tensor_tensor(x_sq[:], x_sb[:], x_sb[:], MULT)
@@ -45,12 +51,12 @@ def tile_loss_kernel(tc, table, x, offs, out):
         acc = [psum.tile([M, PIECE], F32, name=f"acc{p}") for p in range(PIECES)]
         piece_offsets = [offsets[:, p * (PIECE // 16) : (p + 1) * (PIECE // 16)] for p in range(PIECES)]
         for p in range(PIECES):
-            nc.tensor.matmul(acc[p][:], x_sq[:], minus_half[:], start=True, stop=False)
+            nc.tensor.matmul(acc[p][:], x_sq[:], minus_half[:, :PIECE], start=True, stop=False)
         for p in range(PIECES):
             nc.tensor.matmul(acc[p][:], x_sb[:], table_sb[:].indirect(piece_offsets[p]), start=False, stop=False)
         for p in range(PIECES):
             nc.tensor.matmul(
-                acc[p][:], minus_half[:], table_sq[:].indirect(piece_offsets[p]), start=False, stop=True
+                acc[p][:], minus_half[:, :M], table_sq[:].indirect(piece_offsets[p]), start=False, stop=True
             )
 
         dist = held.tile([M, N], F32, name="dist")

@@ -5,13 +5,11 @@ FLOPS = 2 * D * M * N
 BYTES = 2 * D * N + 2 * D * M + 2 * N + 4 * M * N
 
 BF16, F32, U16 = mybir.dt.bfloat16, mybir.dt.float32, mybir.dt.uint16
-MULT, MAX = mybir.AluOpType.mult, mybir.AluOpType.max
+MULT, ADD, MIN = mybir.AluOpType.mult, mybir.AluOpType.add, mybir.AluOpType.min
 SQRT = mybir.ActivationFunctionType.Sqrt
 
-BANK = 512
 PIECE = 128
 PIECES = N // PIECE
-WARM_UP = 8
 SQRT_FLOOR = 2.0**-116
 
 
@@ -21,28 +19,27 @@ def tile_loss_kernel(tc, table, x, offs, out):
         tc.tile_pool(name="held", bufs=1) as held,
         tc.psum_pool(name="psum", bufs=1) as psum,
     ):
+        x_sb = held.tile([D, M], BF16, name="x_sb")
+        nc.sync.dma_start(x_sb[:], x)
         offsets = held.tile([128, N // 16], U16, name="offsets")
         nc.sync.dma_start(offsets[:], offs)
         table_sb = held.tile([D, S], BF16, name="table_sb")
         for h in range(2):
             half = slice(h * (S // 2), (h + 1) * (S // 2))
             nc.scalar.dma_start(table_sb[:, half], table[:, half])
-        x_sb = held.tile([D, M], BF16, name="x_sb")
-        nc.sync.dma_start(x_sb[:], x)
 
-        minus_half = held.tile([D, BANK], BF16, name="minus_half")
+        minus_half = held.tile([D, M], BF16, name="minus_half")
         nc.vector.memset(minus_half[:], -0.5)
 
         scratch = held.tile([128, 1], F32, name="scratch")
         nc.vector.memset(scratch[:], 1.0)
         nc.scalar.activation(scratch[:], scratch[:], SQRT)
 
-        warm = psum.tile([M, BANK], F32, name="warm")
-        for i in range(WARM_UP):
-            nc.tensor.matmul(warm[:], minus_half[:, :M], minus_half[:], start=True, stop=True)
-
         x_sq = held.tile([D, M], BF16, name="x_sq")
         nc.vector.tensor_tensor(x_sq[:], x_sb[:], x_sb[:], MULT)
+        x_norm = psum.tile([M, 1], F32, name="x_norm")
+        nc.tensor.matmul(x_norm[:], x_sq[:], minus_half[:, 0:1], start=True, stop=True)
+
         table_sq = held.tile([D, S], BF16, name="table_sq")
         for h in range(2):
             half = slice(h * (S // 2), (h + 1) * (S // 2))
@@ -51,17 +48,15 @@ def tile_loss_kernel(tc, table, x, offs, out):
         acc = [psum.tile([M, PIECE], F32, name=f"acc{p}") for p in range(PIECES)]
         piece_offsets = [offsets[:, p * (PIECE // 16) : (p + 1) * (PIECE // 16)] for p in range(PIECES)]
         for p in range(PIECES):
-            nc.tensor.matmul(acc[p][:], x_sq[:], minus_half[:, :PIECE], start=True, stop=False)
-        for p in range(PIECES):
-            nc.tensor.matmul(acc[p][:], x_sb[:], table_sb[:].indirect(piece_offsets[p]), start=False, stop=False)
+            nc.tensor.matmul(acc[p][:], x_sb[:], table_sb[:].indirect(piece_offsets[p]), start=True, stop=False)
         for p in range(PIECES):
             nc.tensor.matmul(
-                acc[p][:], minus_half[:, :M], table_sq[:].indirect(piece_offsets[p]), start=False, stop=True
+                acc[p][:], minus_half[:], table_sq[:].indirect(piece_offsets[p]), start=False, stop=True
             )
 
         dist = held.tile([M, N], F32, name="dist")
         for p in range(PIECES):
             columns = slice(p * PIECE, (p + 1) * PIECE)
-            nc.vector.tensor_scalar(dist[:, columns], acc[p][:], -2.0, SQRT_FLOOR, MULT, MAX)
-            nc.scalar.activation(dist[:, columns], dist[:, columns], SQRT)
+            nc.vector.tensor_scalar(dist[:, columns], acc[p][:], x_norm[:, 0:1], -0.5 * SQRT_FLOOR, ADD, MIN)
+            nc.scalar.activation(dist[:, columns], dist[:, columns], SQRT, scale=-2.0)
             nc.sync.dma_start(out[:, columns], dist[:, columns])

@@ -6,10 +6,11 @@ BYTES = 2 * D * N + 2 * D * M + 2 * N + 4 * M * N
 
 BF16, F32, U16 = mybir.dt.bfloat16, mybir.dt.float32, mybir.dt.uint16
 MULT, ADD, MIN = mybir.AluOpType.mult, mybir.AluOpType.add, mybir.AluOpType.min
-SQRT = mybir.ActivationFunctionType.Sqrt
+SQRT, SQUARE = mybir.ActivationFunctionType.Sqrt, mybir.ActivationFunctionType.Square
 
 PIECE = 128
 PIECES = N // PIECE
+SCALAR_FROM = 672
 SQRT_FLOOR = 2.0**-116
 
 
@@ -24,9 +25,7 @@ def tile_loss_kernel(tc, table, x, offs, out):
         offsets = held.tile([128, N // 16], U16, name="offsets")
         nc.sync.dma_start(offsets[:], offs)
         table_sb = held.tile([D, S], BF16, name="table_sb")
-        for h in range(2):
-            half = slice(h * (S // 2), (h + 1) * (S // 2))
-            nc.scalar.dma_start(table_sb[:, half], table[:, half])
+        nc.scalar.dma_start(table_sb[:], table)
 
         minus_half = held.tile([D, M], BF16, name="minus_half")
         nc.vector.memset(minus_half[:], -0.5)
@@ -41,9 +40,9 @@ def tile_loss_kernel(tc, table, x, offs, out):
         nc.tensor.matmul(x_norm[:], x_sq[:], minus_half[:, 0:1], start=True, stop=True)
 
         table_sq = held.tile([D, S], BF16, name="table_sq")
-        for h in range(2):
-            half = slice(h * (S // 2), (h + 1) * (S // 2))
-            nc.vector.tensor_tensor(table_sq[:, half], table_sb[:, half], table_sb[:, half], MULT)
+        for_vector, for_scalar = slice(0, SCALAR_FROM), slice(SCALAR_FROM, S)
+        nc.vector.tensor_tensor(table_sq[:, for_vector], table_sb[:, for_vector], table_sb[:, for_vector], MULT)
+        nc.scalar.activation(table_sq[:, for_scalar], table_sb[:, for_scalar], SQUARE)
 
         acc = [psum.tile([M, PIECE], F32, name=f"acc{p}") for p in range(PIECES)]
         piece_offsets = [offsets[:, p * (PIECE // 16) : (p + 1) * (PIECE // 16)] for p in range(PIECES)]

@@ -1,4 +1,5 @@
 import concourse.mybir as mybir
+from concourse.masks import make_identity
 
 D, S, M, N = 128, 1024, 128, 512
 FLOPS = 2 * D * M * N
@@ -34,15 +35,19 @@ def tile_loss_kernel(tc, table, x, offs, out):
         nc.vector.memset(scratch[:], 1.0)
         nc.scalar.activation(scratch[:], scratch[:], SQRT)
 
-        x_sq = held.tile([D, M], BF16, name="x_sq")
-        nc.vector.tensor_tensor(x_sq[:], x_sb[:], x_sb[:], MULT)
-        x_norm = psum.tile([M, 1], F32, name="x_norm")
-        nc.tensor.matmul(x_norm[:], x_sq[:], minus_half[:, 0:1], start=True, stop=True)
+        identity = held.tile([M, M], F32, name="identity")
+        make_identity(nc, identity[:])
+        pairs = psum.tile([M, M], F32, name="pairs")
+        nc.tensor.matmul(pairs[:], x_sb[:], x_sb[:], start=True, stop=True)
 
         table_sq = held.tile([D, S], BF16, name="table_sq")
         for_vector, for_scalar = slice(0, SCALAR_FROM), slice(SCALAR_FROM, S)
         nc.vector.tensor_tensor(table_sq[:, for_vector], table_sb[:, for_vector], table_sb[:, for_vector], MULT)
         nc.scalar.activation(table_sq[:, for_scalar], table_sb[:, for_scalar], SQUARE)
+
+        diagonal = held.tile([M, M], F32, name="diagonal")
+        x_norm = held.tile([M, 1], F32, name="x_norm")
+        nc.vector.scalar_tensor_tensor(diagonal[:], pairs[:], -0.5, identity[:], MULT, MULT, accum_out=x_norm[:])
 
         acc = [psum.tile([M, PIECE], F32, name=f"acc{p}") for p in range(PIECES)]
         piece_offsets = [offsets[:, p * (PIECE // 16) : (p + 1) * (PIECE // 16)] for p in range(PIECES)]

import concourse.mybir as mybir
from concourse.masks import make_identity

D, S, M, N = 128, 1024, 128, 512
FLOPS = 2 * D * M * N
BYTES = 2 * D * N + 2 * D * M + 2 * N + 4 * M * N

BF16, F32, U16 = mybir.dt.bfloat16, mybir.dt.float32, mybir.dt.uint16
MULT, ADD, MIN = mybir.AluOpType.mult, mybir.AluOpType.add, mybir.AluOpType.min
SQRT, SQUARE = mybir.ActivationFunctionType.Sqrt, mybir.ActivationFunctionType.Square

PIECE = 128
PIECES = N // PIECE
SCALAR_FROM = 672
SQRT_FLOOR = 2.0**-116


def tile_loss_kernel(tc, table, x, offs, out):
    nc = tc.nc
    with (
        tc.tile_pool(name="held", bufs=1) as held,
        tc.psum_pool(name="psum", bufs=1) as psum,
    ):
        x_sb = held.tile([D, M], BF16, name="x_sb")
        nc.sync.dma_start(x_sb[:], x)
        offsets = held.tile([128, N // 16], U16, name="offsets")
        nc.sync.dma_start(offsets[:], offs)
        table_sb = held.tile([D, S], BF16, name="table_sb")
        nc.scalar.dma_start(table_sb[:], table)

        minus_half = held.tile([D, M], BF16, name="minus_half")
        nc.vector.memset(minus_half[:], -0.5)

        scratch = held.tile([128, 1], F32, name="scratch")
        nc.vector.memset(scratch[:], 1.0)
        nc.scalar.activation(scratch[:], scratch[:], SQRT)

        identity = held.tile([M, M], F32, name="identity")
        make_identity(nc, identity[:])
        pairs = psum.tile([M, M], F32, name="pairs")
        nc.tensor.matmul(pairs[:], x_sb[:], x_sb[:], start=True, stop=True)

        table_sq = held.tile([D, S], BF16, name="table_sq")
        for_vector, for_scalar = slice(0, SCALAR_FROM), slice(SCALAR_FROM, S)
        nc.vector.tensor_tensor(table_sq[:, for_vector], table_sb[:, for_vector], table_sb[:, for_vector], MULT)
        nc.scalar.activation(table_sq[:, for_scalar], table_sb[:, for_scalar], SQUARE)

        diagonal = held.tile([M, M], F32, name="diagonal")
        x_norm = held.tile([M, 1], F32, name="x_norm")
        nc.vector.scalar_tensor_tensor(diagonal[:], pairs[:], -0.5, identity[:], MULT, MULT, accum_out=x_norm[:])

        acc = [psum.tile([M, PIECE], F32, name=f"acc{p}") for p in range(PIECES)]
        piece_offsets = [offsets[:, p * (PIECE // 16) : (p + 1) * (PIECE // 16)] for p in range(PIECES)]
        for p in range(PIECES):
            nc.tensor.matmul(acc[p][:], x_sb[:], table_sb[:].indirect(piece_offsets[p]), start=True, stop=False)
        for p in range(PIECES):
            nc.tensor.matmul(
                acc[p][:], minus_half[:], table_sq[:].indirect(piece_offsets[p]), start=False, stop=True
            )

        dist = held.tile([M, N], F32, name="dist")
        for p in range(PIECES):
            columns = slice(p * PIECE, (p + 1) * PIECE)
            nc.vector.tensor_scalar(dist[:, columns], acc[p][:], x_norm[:, 0:1], -0.5 * SQRT_FLOOR, ADD, MIN)
            nc.scalar.activation(dist[:, columns], dist[:, columns], SQRT, scale=-2.0)
            nc.sync.dma_start(out[:, columns], dist[:, columns])
